import numpy as np
import ml_dtypes


def mxq(x, axis, fmt="e4m3"):
    dtype, down = {"e4m3": (ml_dtypes.float8_e4m3fn, 7), "e5m2": (ml_dtypes.float8_e5m2, 14)}[fmt]
    v = np.moveaxis(np.asarray(x, np.float32).astype(ml_dtypes.bfloat16).astype(np.float64), axis, -1)
    blocks = v.reshape(v.shape[:-1] + (-1, 32))
    amax = np.abs(blocks).max(-1, keepdims=True)
    byte = np.maximum(np.where(amax > 0, np.frexp(amax)[1] - 1 + 127, 0) - down, 1)
    scale = np.exp2(byte - 127.0)
    codes = (blocks / scale).astype(np.float32).astype(dtype).astype(np.float64)
    return np.moveaxis((codes * scale).reshape(v.shape), -1, axis)


WIDE = False


def mx_kscale(k):
    if not WIDE:
        return np.ones(k)
    levels = np.array([10, -10, 5, -5, 0])
    if k % 512:
        return np.exp2(np.random.permutation(np.resize(levels, k // 32))).repeat(32)
    a = np.empty((k // 512, 16))
    for p in range(k // 512):
        a[p, :8] = np.random.permutation(np.resize(levels, 8))
        for g in range(8):
            far = levels[np.abs(levels - a[p, g]) >= 10]
            a[p, g + 8] = far[np.random.randint(len(far))]
    return np.exp2(a.ravel()).repeat(32)


BF16 = ml_dtypes.bfloat16


def bf(x):
    return np.asarray(x, np.float32).astype(BF16)


def f64(x):
    return np.asarray(x).astype(np.float64)


E2M1 = np.array([0.0, 0.5, 1.0, 1.5, 2.0, 3.0, 4.0, 6.0, -0.0, -0.5, -1.0, -1.5, -2.0, -3.0, -4.0, -6.0])


def pack_weight(w, fmt):
    k, n = w.shape
    w = f64(bf(w)).reshape(k // 32, 32, n)
    amax = np.abs(w).max(1)
    if fmt == "e4m3":
        byte = np.frexp(amax)[1] - 1 + 127 - 7
    else:
        mant, ex = np.frexp(amax / 6.0)
        byte = np.where(mant > 0.5, ex, ex - 1) + 127
    byte = np.clip(np.where(amax > 0, byte, 1), 1, 254)
    scaled = (w * np.exp2(127.0 - byte)[:, None, :]).reshape(k, n).astype(np.float32)
    by_word = np.ascontiguousarray(scaled.reshape(k // 512, 128, 4, n).transpose(0, 1, 3, 2))
    if fmt == "e4m3":
        words = by_word.astype(ml_dtypes.float8_e4m3fn).view(np.uint8)
    else:
        c = by_word.astype(ml_dtypes.float4_e2m1fn).view(np.uint8) & 0xF
        words = c[..., 0::2] | (c[..., 1::2] << 4)
    return np.ascontiguousarray(words), np.ascontiguousarray(byte.astype(np.uint8).reshape(k // 512, 16, n))


def unpack_weight(words, scales, fmt):
    g, p, n, _ = words.shape
    if fmt == "e4m3":
        vals = np.ascontiguousarray(words).view(ml_dtypes.float8_e4m3fn).astype(np.float64)
    else:
        nib = np.empty((g, p, n, 4), np.uint8)
        nib[..., 0::2] = words & 0xF
        nib[..., 1::2] = words >> 4
        vals = E2M1[nib]
    vals = vals * np.repeat(np.exp2(scales.astype(np.float64) - 127.0), 8, axis=1)[..., None]
    return vals.transpose(0, 1, 3, 2).reshape(g * 512, n)
def pack4(w):
    words, scales = pack_weight(w, "e2m1")
    return words.reshape(words.shape[0], 128, -1), scales


def unpack4(words, scales):
    return unpack_weight(words.reshape(words.shape[0], 128, -1, 2), scales, "e2m1")


B, S, D, E, WINDOW = 8, 512, 1024, 512, 10
HALF = WINDOW // 2


def draw0():
    s, t = mx_kscale(D), mx_kscale(E)
    x = bf(np.random.standard_normal((B, S, D)) * s)
    Wq = np.random.standard_normal((E, D)) / np.sqrt(D) / s[None, :] * t[:, None]
    words, scales = pack4(Wq.T)
    return {"x": x,
            "Wq_words": words,
            "Wq_scales": scales,
            "bq": bf(np.random.standard_normal(E) * 0.1 * t),
            "k": bf(np.random.standard_normal((B, S, E)) / t)}


def core(x, Wq_words, Wq_scales, bq, k):
    q = (mxq(f64(x), 2, "e4m3") @ unpack4(Wq_words, Wq_scales)) + f64(bq)
    scores = (mxq(q, 2, "e4m3") @ mxq(f64(k), 2, "e4m3").transpose(0, 2, 1)) / np.sqrt(E)
    i = np.arange(S)[:, None]
    j = np.arange(S)[None, :]
    mask = np.abs(i - j) <= HALF
    scores = np.where(mask[None, :, :], scores, -1e9)
    e = np.exp(scores - scores.max(-1, keepdims=True))
    return e / e.sum(-1, keepdims=True)


def e4m3fn_bytes(y):
    return np.clip(np.asarray(y, np.float64), -448.0, 448.0).astype(np.float32).astype(ml_dtypes.float8_e4m3fn).view(np.uint8)


def e4m3fn_values(b):
    return np.asarray(b, np.uint8).view(ml_dtypes.float8_e4m3fn).astype(np.float64)


def setup_inputs():
    d = draw0()
    x0 = np.asarray(d['x']).astype(np.float64)
    s = (np.max(np.abs(x0), axis=(0, 1), keepdims=True) / 448.0).astype(np.float32)
    out = {}
    for k, v in d.items():
        if k == 'x':
            out['x_bytes'] = e4m3fn_bytes(x0 / s.astype(np.float64))
            out['x_scale'] = s
        else:
            out[k] = v
    return out


def reference(x_bytes, x_scale, Wq_words, Wq_scales, bq, k):
    return core(e4m3fn_values(x_bytes) * x_scale.astype(np.float64), Wq_words, Wq_scales, bq, k)

import math
from contextlib import ExitStack

import concourse.mybir as mybir
from concourse.masks import make_identity

B, S, D, E = 8, 512, 1024, 512
HALF = 5
FLOPS = 2 * B * S * D * E + 2 * B * S * S * E

F32 = mybir.dt.float32
BF16 = mybir.dt.bfloat16
I32 = mybir.dt.int32
U32 = mybir.dt.uint32
U8 = mybir.dt.uint8
FP8 = mybir.dt.float8_e4m3fn
FP8X4 = mybir.dt.float8_e4m3fn_x4
FP4X4 = mybir.dt.float4_e2m1fn_x4
ALU = mybir.AluOpType
ACT = mybir.ActivationFunctionType
AX = mybir.AxisListType

P = 128
NT = S // P
BAND = P + 2 * HALF
EDGE = P + HALF
KEYS = 256
SCALE = 1.0 / math.sqrt(E)


def tile_localattention_pa_t_w4_kernel(tc, x_bytes, x_scale, Wq_words, Wq_scales, bq, k, out):
    nc = tc.nc
    with ExitStack() as ctx:
        keep = ctx.enter_context(tc.tile_pool(name="keep", bufs=1))
        load = ctx.enter_context(tc.tile_pool(name="load", bufs=8))
        work = ctx.enter_context(tc.tile_pool(name="work", bufs=2))
        psum = ctx.enter_context(tc.psum_pool(name="psum", bufs=3))

        ident = keep.tile([P, P], F32, name="ident")
        scale_b = keep.tile([P, D], F32, name="scale_b", align_bytes=64)
        w_raw = keep.tile([P, 2, 2 * E], U8, name="w_raw", align_bytes=64)
        w_perm = keep.tile([P, 2, 2 * E], U8, name="w_perm", align_bytes=64)
        ws_raw = keep.tile([P, 2, E], U8, name="ws_raw", align_bytes=64)
        ws_perm = keep.tile([P, 2, E], U8, name="ws_perm", align_bytes=64)
        bias = keep.tile([P, 4], BF16, name="bias")
        mask_in = keep.tile([P, 2, BAND], F32, name="mask_in")
        mask_edge = keep.tile([P, 2, EDGE], F32, name="mask_edge")
        warm = keep.tile([P, 1], F32, name="warm")
        stages = [keep.tile([P, NT, S], F32, name=f"stage{i}") for i in range(3)]

        x_tiles = [load.tile([P, NT, D], U8, name="x_codes", align_bytes=64) for b in range(B)]
        k_tiles = [load.tile([P, NT, E], BF16, name="k_rows", align_bytes=64) for b in range(B)]

        xs = x_scale.rearrange("a b k -> (a b k)")
        xv = x_bytes.rearrange("b (i p) k -> b p i k", p=P)
        kv = k.rearrange("b (i p) e -> b p i e", p=P)
        ov = out.rearrange("b (i p) j -> b p i j", p=P)

        nc.sync.dma_start(out=x_tiles[0][:, 0, :], in_=xv[0][:, 0, :])
        nc.scalar.dma_start(out=scale_b[:, 0:512], in_=xs[0:512].partition_broadcast(P))
        nc.scalar.dma_start(out=scale_b[:, 512:1024], in_=xs[512:1024].partition_broadcast(P))
        nc.scalar.dma_start(out=bias[:], in_=bq.rearrange("(p t) -> p t", t=4))
        nc.gpsimd.memset(ws_raw[:].rearrange("p g n -> p (g n)").bitcast(I32), 0)
        nc.sync.dma_start(out=w_raw[:], in_=Wq_words.rearrange("g p n -> p g n"))
        nc.sync.dma_start(out=x_tiles[0][:, 1:4, :], in_=xv[0][:, 1:4, :])
        nc.sync.dma_start(out=k_tiles[0][:], in_=kv[0])
        for q in range(4):
            nc.sync.dma_start(
                out=ws_raw[32 * q : 32 * q + 4].bitcast(I32),
                in_=Wq_scales[:, 4 * q : 4 * q + 4, :].rearrange("g r n -> r g n").bitcast(I32),
            )
        for b in range(1, B):
            nc.sync.dma_start(out=x_tiles[b][:], in_=xv[b])
            nc.sync.dma_start(out=k_tiles[b][:], in_=kv[b])

        make_identity(nc, ident[:])
        nc.vector.memset(warm[:], 0.0)
        nc.scalar.activation(out=warm[:], in_=warm[:], func=ACT.Exp)
        nc.vector.memset(stages[0][:], 0.0)
        nc.gpsimd.memset(mask_in[:], 0.0)
        m0 = mask_in[:, 0, :]
        nc.gpsimd.affine_select(out=m0, in_=m0, pattern=[[1, BAND]], compare_op=ALU.is_ge, fill=-1e9, base=0, channel_multiplier=-1)
        nc.gpsimd.affine_select(out=m0, in_=m0, pattern=[[-1, BAND]], compare_op=ALU.is_ge, fill=-1e9, base=2 * HALF, channel_multiplier=1)
        nc.gpsimd.tensor_copy(out=mask_in[:, 1, :], in_=mask_in[:, 0, :])
        nc.gpsimd.tensor_copy(out=mask_edge[:, 0, :], in_=mask_in[:, 0, 0:EDGE])
        nc.gpsimd.tensor_copy(out=mask_edge[:, 1, :], in_=mask_in[:, 0, HALF:BAND])
        nc.gpsimd.memset(stages[1][:], 0.0)
        nc.gpsimd.memset(stages[2][:], 0.0)

        xi, xc, xsc, kc, ksc, qp, qi, qc, qsc, xw, kt = {}, {}, {}, {}, {}, {}, {}, {}, {}, {}, {}
        sm, st = {}, {}

        def widen(u, i):
            w = work.tile([P, D], BF16, name="xw", bufs=4, align_bytes=64)
            xw[u, i] = w
            halves = 2 if (u, i) == (0, 0) else 1
            n = D // halves
            for h in range(halves):
                nc.vector.tensor_tensor(
                    out=w[:, n * h : n * (h + 1)],
                    in0=x_tiles[u][:, i, n * h : n * (h + 1)].bitcast(FP8),
                    in1=scale_b[:, n * h : n * (h + 1)],
                    op=ALU.mult,
                )

        def xpose(u, i):
            if i == 0:
                xi[u] = work.tile([P, 2, S, 2], F32, name="xi", align_bytes=64)
            words = xw[u, i][:].bitcast(F32)
            tp = psum.tile([P, 2, 2, P], F32, name="tp")
            for g in range(2):
                for h in range(2):
                    nc.tensor.transpose(tp[:, g, h, :], words[:, 256 * g + h : 256 * (g + 1) : 2], ident[:])
            nc.scalar.copy(out=xi[u][:, :, P * i : P * (i + 1), :], in_=tp[:].rearrange("p g h r -> p g r h"))

        def quant_x(u):
            xc[u] = work.tile([P, 2, S], U32, name="xc", align_bytes=64)
            xsc[u] = work.tile([P, 2, S], U8, name="xsc", align_bytes=64)
            for g in range(2):
                nc.vector.quantize_mx(
                    out=xc[u][:, g, :].bitcast(FP8X4),
                    scales=xsc[u][:, g, :],
                    in_=xi[u][:, g].rearrange("p n h -> p (n h)").bitcast(BF16),
                )

        def kpose(b, half):
            if half == 0:
                kt[b] = work.tile([P, S, 2], F32, name="kt", align_bytes=64)
            tp = psum.tile([P, 2, 2, P], F32, name="tp")
            for j in range(2):
                words = k_tiles[b][:, 2 * half + j, :].bitcast(F32)
                for h in range(2):
                    nc.tensor.transpose(tp[:, j, h, :], words[:, h:256:2], ident[:])
            dst = kt[b][:, 256 * half : 256 * (half + 1), :].rearrange("p (j r) h -> p j r h", j=2)
            nc.scalar.copy(out=dst, in_=tp[:].rearrange("p j h r -> p j r h"))

        def quant_k(b):
            kc[b] = work.tile([P, S], U32, name="kc", bufs=3, align_bytes=64)
            ksc[b] = work.tile([P, S], U8, name="ksc", bufs=3, align_bytes=64)
            nc.vector.quantize_mx(
                out=kc[b][:].bitcast(FP8X4),
                scales=ksc[b][:],
                in_=kt[b][:].rearrange("p n h -> p (n h)").bitcast(BF16),
            )

        def project(u, t):
            if t == 0:
                qp[u] = work.tile([P, 2, S], F32, name="qp", align_bytes=64)
            acc = psum.tile([P, S], F32, name="acc")
            for g in range(2):
                nc.tensor.matmul_mx(
                    out=acc[:],
                    lhsT=w_perm[:, g, 256 * t : 256 * (t + 1)].bitcast(FP4X4),
                    lhsT_scale=ws_perm[:, g, P * t : P * (t + 1)],
                    rhs=xc[u][:, g, :].bitcast(FP8X4),
                    rhs_scale=xsc[u][:, g, :],
                    start=(g == 0),
                    stop=(g == 1),
                )
            pair = qp[u][:, t // 2, :].bitcast(BF16)
            nc.scalar.activation(out=pair[:, t % 2 :: 2], in_=acc[:], func=ACT.Identity, bias=bias[:, t : t + 1])

        def interleave(u):
            qi[u] = work.tile([P, S, 2], F32, name="qi", align_bytes=64)
            nc.vector.tensor_copy(out=qi[u][:], in_=qp[u][:].rearrange("p h n -> p n h"))

        def quant_q(u):
            qc[u] = work.tile([P, S], U32, name="qc", align_bytes=64)
            qsc[u] = work.tile([P, S], U8, name="qsc", align_bytes=64)
            nc.vector.quantize_mx(
                out=qc[u][:].bitcast(FP8X4),
                scales=qsc[u][:],
                in_=qi[u][:].rearrange("p n h -> p (n h)").bitcast(BF16),
            )

        PAIRS = (((1, 64), (2, 192)), ((3, 256), (0, 0)))

        def scores(u, pair):
            sc = psum.tile([P, 2, KEYS], F32, name="sc", bufs=2)
            for h in range(2):
                i, j0 = PAIRS[pair][h]
                nc.tensor.matmul_mx(
                    out=sc[:, h, :],
                    lhsT=qc[u][:, P * i : P * (i + 1)].bitcast(FP8X4),
                    lhsT_scale=qsc[u][:, P * i : P * (i + 1)],
                    rhs=kc[u][:, j0 : j0 + KEYS].bitcast(FP8X4),
                    rhs_scale=ksc[u][:, j0 : j0 + KEYS],
                    start=True,
                    stop=True,
                )
            if pair == 0:
                width = BAND
                m = work.tile([P, 2, BAND], F32, name="m0", bufs=3)
                src, dst, msk = sc[:, :, 59 : 59 + BAND], m[:], mask_in[:]
            else:
                width = EDGE
                m = work.tile([P, 2, EDGE], F32, name="m1", bufs=3)
                src = sc[:].rearrange("p h j -> p (h j)")[:, 256 - EDGE : 256 + EDGE]
                dst, msk = m[:].rearrange("p h j -> p (h j)"), mask_edge[:].rearrange("p h j -> p (h j)")
            nc.vector.scalar_tensor_tensor(out=dst, in0=src, scalar=SCALE, in1=msk, op0=ALU.mult, op1=ALU.add)
            nm = work.tile([P, 2], F32, name="nm", bufs=4)
            sm[u, pair] = (m, nm)

        def rowmax(u, pair):
            m, nm = sm[u, pair]
            nc.vector.tensor_reduce(out=nm[:], in_=m[:], axis=AX.X, op=ALU.max, negate=True)

        def exps(u, pair):
            m, nm = sm[u, pair]
            ss = work.tile([P, 2], F32, name="ss", bufs=4)
            for h in range(2):
                nc.scalar.activation(out=m[:, h, :], in_=m[:, h, :], func=ACT.Exp, bias=nm[:, h : h + 1], accum_out=ss[:, h : h + 1])
            st[u, pair] = ss

        def finish(u, pair):
            m, nm = sm[u, pair]
            rs = work.tile([P, 2], F32, name="rs", bufs=4)
            nc.vector.reciprocal(out=rs[:], in_=st[u, pair][:])
            stage = stages[u % 3]
            for h in range(2):
                i = PAIRS[pair][h][0]
                lo = max(0, P * i - HALF)
                hi = min(S, P * (i + 1) + HALF)
                nc.scalar.activation(out=stage[:, i, lo:hi], in_=m[:, h, :], func=ACT.Copy, scale=rs[:, h : h + 1])
            tiles = slice(1, 3) if pair == 0 else slice(0, 4, 3)
            nc.sync.dma_start(out=ov[u][:, tiles, :], in_=stage[:, tiles, :])

        for s in range(B + 2):
            new, mid, old = s < B, 0 <= s - 1 < B, 0 <= s - 2 < B
            if new:
                widen(s, 0)
                xpose(s, 0)
            if mid:
                quant_x(s - 1)
                project(s - 1, 0)
                project(s - 1, 1)
            if old:
                scores(s - 2, 0)
            if new:
                widen(s, 1)
                xpose(s, 1)
            if old:
                rowmax(s - 2, 0)
                exps(s - 2, 0)
                scores(s - 2, 1)
            if mid:
                project(s - 1, 2)
                project(s - 1, 3)
            if new:
                kpose(s, 0)
                widen(s, 2)
                xpose(s, 2)
            if s == 0:
                for g in range(2):
                    nc.vector.tensor_copy(
                        out=w_perm[:, g, :].rearrange("p (t m c) -> p m t c", t=4, c=2),
                        in_=w_raw[:, g, :].rearrange("p (m t c) -> p m t c", t=4, c=2),
                    )
                    nc.vector.tensor_copy(
                        out=ws_perm[:, g, :].rearrange("p (t m) -> p m t", t=4),
                        in_=ws_raw[:, g, :].rearrange("p (m t) -> p m t", t=4),
                    )
            if old:
                rowmax(s - 2, 1)
                finish(s - 2, 0)
                exps(s - 2, 1)
            if new:
                kpose(s, 1)
            if mid:
                interleave(s - 1)
            if new:
                widen(s, 3)
                xpose(s, 3)
                quant_k(s)
            if old:
                finish(s - 2, 1)
            if mid:
                quant_q(s - 1)
